import numpy as np
import ml_dtypes


def mxq(x, axis, fmt="e4m3"):
    dtype, down = {"e4m3": (ml_dtypes.float8_e4m3fn, 7), "e5m2": (ml_dtypes.float8_e5m2, 14)}[fmt]
    v = np.moveaxis(np.asarray(x, np.float32).astype(ml_dtypes.bfloat16).astype(np.float64), axis, -1)
    blocks = v.reshape(v.shape[:-1] + (-1, 32))
    amax = np.abs(blocks).max(-1, keepdims=True)
    byte = np.maximum(np.where(amax > 0, np.frexp(amax)[1] - 1 + 127, 0) - down, 1)
    scale = np.exp2(byte - 127.0)
    codes = (blocks / scale).astype(np.float32).astype(dtype).astype(np.float64)
    return np.moveaxis((codes * scale).reshape(v.shape), -1, axis)


WIDE = False


def mx_kscale(k):
    if not WIDE:
        return np.ones(k)
    levels = np.array([10, -10, 5, -5, 0])
    a = np.random.permutation(np.resize(levels, k // 512 * 4)).reshape(k // 512, 4)
    idx = np.arange(k)
    return np.exp2(a[idx // 512, idx % 128 // 32])


BF16 = ml_dtypes.bfloat16


def bf(x):
    return np.asarray(x, np.float32).astype(BF16)


def f64(x):
    return np.asarray(x).astype(np.float64)


B, S, D, H, KV, HD = 2, 256, 2048, 16, 8, 128
HALF = HD // 2
ROPE_BASE = 1.0e4


def rotate_half(t):
    return np.concatenate((-t[..., HALF:], t[..., :HALF]), axis=-1)


def setup_inputs():
    s = mx_kscale(D)
    inv_freq = 1.0 / ROPE_BASE ** (np.arange(HALF) / HALF)
    freqs = np.outer(np.arange(S), inv_freq)
    emb = np.concatenate((freqs, freqs), axis=-1)
    w = 1.0 / np.sqrt(D)
    return {"x": bf(np.random.standard_normal((B, S, D)) * s),
            "cos": bf(np.cos(emb)),
            "sin": bf(np.sin(emb)),
            "Wq": bf(np.random.standard_normal((D, H * HD)) * w / s[:, None]),
            "Wk": bf(np.random.standard_normal((D, KV * HD)) * w / s[:, None]),
            "Wv": bf(np.random.standard_normal((D, KV * HD)) * w / s[:, None])}


def reference(x, cos, sin, Wq, Wk, Wv):
    xq = mxq(f64(x), 2, "e4m3")
    q = (xq @ mxq(f64(Wq), 0, "e4m3")).reshape(B, S, H, HD)
    k = (xq @ mxq(f64(Wk), 0, "e4m3")).reshape(B, S, KV, HD)
    v = (xq @ mxq(f64(Wv), 0, "e4m3")).reshape(B, S, KV, HD)
    c = f64(cos)[None, :, None, :]
    sn = f64(sin)[None, :, None, :]
    q_rot = q * c + rotate_half(q) * sn
    k_rot = k * c + rotate_half(k) * sn
    return q_rot, k_rot, v

@@ -1,0 +1,228 @@
+from contextlib import ExitStack
+
+import concourse.mybir as mybir
+from concourse.masks import make_identity
+
+F32 = mybir.dt.float32
+BF16 = mybir.dt.bfloat16
+U32 = mybir.dt.uint32
+U8 = mybir.dt.uint8
+FP8X4 = mybir.dt.float8_e4m3fn_x4
+MULT = mybir.AluOpType.mult
+ADD = mybir.AluOpType.add
+
+P = 128
+PACK = 4
+K_PASS = P * PACK
+TOKENS = 512
+D_MODEL = 2048
+PASSES = D_MODEL // K_PASS
+TOKEN_TILES = TOKENS // P
+POSITION_TILES = 256 // P
+HEAD = 128
+HALF = HEAD // 2
+GROUP_COLS = 512
+GROUP_HEADS = GROUP_COLS // HEAD
+WORDS_PER_PASS = K_PASS // 2
+
+FLOPS = 2 * TOKENS * D_MODEL * (2048 + 1024 + 1024)
+
+PREFETCH = 6
+MULTIPLY_LAG = 1
+FINISH_LAG = PASSES + MULTIPLY_LAG
+
+IDLE_VECTOR_COLS = 256
+
+
+def tile_attention_pa_kernel(tc, x, cos, sin, Wq, Wk, Wv, out_0, out_1, out_2):
+    nc = tc.nc
+
+    groups = []
+    for weight, result_4d, with_rope in ((Wq, out_0, True), (Wk, out_1, True), (Wv, out_2, False)):
+        result_rows = result_4d.rearrange("b s h d -> (b s) (h d)")
+        for col0 in range(0, weight.shape[1], GROUP_COLS):
+            groups.append((weight, result_rows, col0, with_rope))
+    n_chunks = len(groups) * PASSES
+    n_banks = len(groups) * TOKEN_TILES
+
+    with ExitStack() as ctx:
+        ctx.enter_context(tc.manual_schedule())
+        const = ctx.enter_context(tc.tile_pool(name="const", bufs=1))
+        x_pool = ctx.enter_context(tc.tile_pool(name="x_rows", bufs=TOKEN_TILES))
+        raw_pool = ctx.enter_context(tc.tile_pool(name="raw", bufs=PREFETCH + 2))
+        grouped_pool = ctx.enter_context(tc.tile_pool(name="grouped", bufs=4))
+        codes_pool = ctx.enter_context(tc.tile_pool(name="codes", bufs=6))
+        rope_pool = ctx.enter_context(tc.tile_pool(name="rope", bufs=3))
+        result_pool = ctx.enter_context(tc.tile_pool(name="result", bufs=4))
+        psum = ctx.enter_context(tc.psum_pool(name="psum", bufs=8))
+
+        x_rows = x.rearrange("b s k -> (b s) k")
+        x_tiles = []
+        for tt in range(TOKEN_TILES):
+            x_sb = x_pool.tile([P, D_MODEL], BF16, name="x_sb")
+            nc.sync.dma_start(out=x_sb[:], in_=x_rows[tt * P : (tt + 1) * P, :])
+            x_tiles.append(x_sb)
+
+        cos_bf = const.tile([P, POSITION_TILES, HEAD], BF16, name="cos_bf")
+        sin_bf = const.tile([P, POSITION_TILES, HEAD], BF16, name="sin_bf")
+        nc.scalar.dma_start(out=cos_bf[:], in_=cos.rearrange("(h p) d -> p h d", p=P))
+        nc.scalar.dma_start(out=sin_bf[:], in_=sin.rearrange("(h p) d -> p h d", p=P))
+
+        raw_tiles = {}
+
+        def load(chunk):
+            weight, col0 = groups[chunk // PASSES][0], groups[chunk // PASSES][2]
+            k0 = (chunk % PASSES) * K_PASS
+            raw = raw_pool.tile([P, PACK, GROUP_COLS], BF16, name="raw")
+            nc.sync.dma_start(
+                out=raw[:],
+                in_=weight[k0 : k0 + K_PASS, col0 : col0 + GROUP_COLS].rearrange(
+                    "(p j) w -> p j w", j=PACK
+                ),
+            )
+            raw_tiles[chunk] = raw
+
+        for chunk in range(PREFETCH):
+            load(chunk)
+
+        identity = const.tile([P, P], F32, name="identity")
+        make_identity(nc, identity[:])
+
+        cos_f32 = const.tile([P, POSITION_TILES, HEAD], F32, name="cos_f32")
+        sin_signed = const.tile([P, POSITION_TILES, HEAD], F32, name="sin_signed")
+        nc.vector.tensor_copy(out=cos_f32[:], in_=cos_bf[:])
+        nc.vector.tensor_scalar_mul(
+            out=sin_signed[:, :, 0:HALF], in0=sin_bf[:, :, 0:HALF], scalar1=-1.0
+        )
+        nc.vector.tensor_copy(out=sin_signed[:, :, HALF:HEAD], in_=sin_bf[:, :, HALF:HEAD])
+
+        x_grouped = const.tile([P, TOKEN_TILES, PASSES, P, 2], F32, name="x_grouped", align_bytes=64)
+        x_codes = const.tile([P, TOKEN_TILES, PASSES, P], U32, name="x_codes", align_bytes=64)
+        x_scales = const.tile([P, TOKEN_TILES, PASSES, P], U8, name="x_scales", align_bytes=64)
+
+        def quantise_x(tt):
+            nc.vector.quantize_mx(
+                out=x_codes[:, tt].rearrange("p c t -> p (c t)").bitcast(FP8X4),
+                scales=x_scales[:, tt].rearrange("p c t -> p (c t)"),
+                in_=x_grouped[:, tt].rearrange("p c t u -> p (c t u)").bitcast(BF16),
+            )
+
+        for tt in range(TOKEN_TILES):
+            x_words = x_tiles[tt][:].bitcast(F32)
+            for first_pass, copy_out in ((0, nc.scalar.copy), (2, nc.vector.tensor_copy)):
+                x_t = psum.tile([P, 2, 2, P], F32, name="x_t", tag="bank")
+                for c2 in range(2):
+                    w0 = (first_pass + c2) * WORDS_PER_PASS
+                    for u in range(2):
+                        nc.tensor.transpose(
+                            out=x_t[:, c2, u, :],
+                            in_=x_words[:, w0 + u : w0 + WORDS_PER_PASS : 2],
+                            identity=identity[:],
+                        )
+                copy_out(
+                    out=x_grouped[:, tt, first_pass : first_pass + 2],
+                    in_=x_t[:].rearrange("p c u t -> p c t u"),
+                )
+            if tt > 0:
+                quantise_x(tt - 1)
+        quantise_x(TOKEN_TILES - 1)
+
+        grouped_tiles = {}
+        bank_tiles = {}
+
+        def has_rope(slot):
+            bank = slot - FINISH_LAG
+            return 0 <= bank < n_banks and groups[bank // TOKEN_TILES][3]
+
+        def regroup(chunk, vector_cols):
+            raw = raw_tiles[chunk]
+            grouped = grouped_pool.tile([P, GROUP_COLS, PACK], BF16, name="grouped", align_bytes=64)
+            scalar_cols = GROUP_COLS - vector_cols
+            for copy, w0, w1 in (
+                (nc.scalar.copy, 0, scalar_cols),
+                (nc.vector.tensor_copy, scalar_cols, GROUP_COLS),
+            ):
+                if w1 > w0:
+                    copy(
+                        out=grouped[:, w0:w1, :].rearrange("p (r i) j -> p r j i", i=4),
+                        in_=raw[:, :, w0:w1].rearrange("p j (r i) -> p r j i", i=4),
+                    )
+            grouped_tiles[chunk] = grouped
+
+        def quantise_and_multiply(chunk):
+            group, c = divmod(chunk, PASSES)
+            grouped = grouped_tiles[chunk]
+            w_codes = codes_pool.tile([P, GROUP_COLS], U32, name="w_codes", align_bytes=64)
+            w_scales = codes_pool.tile([P, GROUP_COLS], U8, name="w_scales", align_bytes=64)
+            nc.vector.quantize_mx(
+                out=w_codes[:].bitcast(FP8X4),
+                scales=w_scales[:],
+                in_=grouped[:].rearrange("p w j -> p (w j)"),
+            )
+            for tt in range(TOKEN_TILES):
+                if c == 0:
+                    bank = psum.tile([P, GROUP_COLS], F32, name="bank", tag="bank")
+                    bank_tiles[group * TOKEN_TILES + tt] = bank
+                nc.tensor.matmul_mx(
+                    out=bank_tiles[group * TOKEN_TILES + tt][:],
+                    lhsT=x_codes[:, tt, c, :].bitcast(FP8X4),
+                    lhsT_scale=x_scales[:, tt, c, :],
+                    rhs=w_codes[:].bitcast(FP8X4),
+                    rhs_scale=w_scales[:],
+                    start=(c == 0),
+                    stop=(c == PASSES - 1),
+                )
+
+        def rope_products(index):
+            bank = bank_tiles[index]
+            pt = (index % TOKEN_TILES) % POSITION_TILES
+            direct = rope_pool.tile([P, GROUP_HEADS, HEAD], F32, name="direct")
+            crossed = rope_pool.tile([P, GROUP_HEADS, 2, HALF], F32, name="crossed")
+            nc.vector.tensor_tensor(
+                out=direct[:],
+                in0=bank[:].rearrange("p (h d) -> p h d", d=HEAD),
+                in1=cos_f32[:, pt, :].unsqueeze(1).to_broadcast([P, GROUP_HEADS, HEAD]),
+                op=MULT,
+            )
+            halves = bank[:].rearrange("p (h two d) -> p h two d", two=2, d=HALF)
+            for two in range(2):
+                nc.vector.tensor_tensor(
+                    out=crossed[:, :, two, :],
+                    in0=halves[:, :, 1 - two, :],
+                    in1=sin_signed[:, pt, two * HALF : (two + 1) * HALF]
+                    .unsqueeze(1)
+                    .to_broadcast([P, GROUP_HEADS, HALF]),
+                    op=MULT,
+                )
+            return direct, crossed
+
+        def store(index, result):
+            result_rows, col0 = groups[index // TOKEN_TILES][1], groups[index // TOKEN_TILES][2]
+            t0 = (index % TOKEN_TILES) * P
+            nc.sync.dma_start(out=result_rows[t0 : t0 + P, col0 : col0 + GROUP_COLS], in_=result[:])
+
+        for slot in range(n_banks + FINISH_LAG):
+            if slot + PREFETCH < n_chunks:
+                load(slot + PREFETCH)
+            if slot < n_chunks:
+                regroup(slot, 0 if has_rope(slot) else IDLE_VECTOR_COLS)
+
+            index = slot - FINISH_LAG
+            if has_rope(slot):
+                direct, crossed = rope_products(index)
+            if 0 <= slot - MULTIPLY_LAG < n_chunks:
+                quantise_and_multiply(slot - MULTIPLY_LAG)
+            if index >= 0:
+                result = result_pool.tile([P, GROUP_COLS], F32, name="result")
+                if has_rope(slot):
+                    nc.vector.tensor_tensor(
+                        out=result[:],
+                        in0=direct[:].rearrange("p h d -> p (h d)"),
+                        in1=crossed[:].rearrange("p h two d -> p (h two d)"),
+                        op=ADD,
+                    )
+                elif index % 2 == 0:
+                    nc.scalar.copy(out=result[:], in_=bank_tiles[index][:])
+                else:
+                    nc.vector.tensor_copy(out=result[:], in_=bank_tiles[index][:])
+                store(index, result)

@@ -28,10 +28,11 @@ WORDS_PER_PASS = K_PASS // 2
 FLOPS = 2 * TOKENS * D_MODEL * (2048 + 1024 + 1024)
 
 PREFETCH = 6
-MULTIPLY_LAG = 1
+MULTIPLY_LAG = 2
 FINISH_LAG = PASSES + MULTIPLY_LAG
 
 IDLE_VECTOR_COLS = 256
+BUSY_VECTOR_COLS = 64
 
 
 def tile_attention_pa_kernel(tc, x, cos, sin, Wq, Wk, Wv, out_0, out_1, out_2):
@@ -204,18 +205,17 @@ def tile_attention_pa_kernel(tc, x, cos, sin, Wq, Wk, Wv, out_0, out_1, out_2):
         for slot in range(n_banks + FINISH_LAG):
             if slot + PREFETCH < n_chunks:
                 load(slot + PREFETCH)
-            if slot < n_chunks:
-                regroup(slot, 0 if has_rope(slot) else IDLE_VECTOR_COLS)
-
-            index = slot - FINISH_LAG
-            if has_rope(slot):
-                direct, crossed = rope_products(index)
             if 0 <= slot - MULTIPLY_LAG < n_chunks:
                 quantise_and_multiply(slot - MULTIPLY_LAG)
+            if slot < n_chunks:
+                regroup(slot, BUSY_VECTOR_COLS if has_rope(slot) else IDLE_VECTOR_COLS)
+
+            index = slot - FINISH_LAG
             if index >= 0:
                 result = result_pool.tile([P, GROUP_COLS], F32, name="result")
                 if has_rope(slot):
-                    nc.vector.tensor_tensor(
+                    direct, crossed = rope_products(index)
+                    nc.gpsimd.tensor_tensor(
                         out=result[:],
                         in0=direct[:].rearrange("p h d -> p (h d)"),
                         in1=crossed[:].rearrange("p h two d -> p (h two d)"),

@@ -23,13 +23,14 @@ HEAD = 128
 HALF = HEAD // 2
 GROUP_COLS = 512
 GROUP_HEADS = GROUP_COLS // HEAD
+PAIR_COLS = 2 * GROUP_COLS
 WORDS_PER_PASS = K_PASS // 2
 
 FLOPS = 2 * TOKENS * D_MODEL * (2048 + 1024 + 1024)
 
-PREFETCH = 6
+PREFETCH = 2 * PASSES
 MULTIPLY_LAG = 2
-FINISH_LAG = PASSES + MULTIPLY_LAG
+FINISH_LAG = 2 * PASSES - 2 + MULTIPLY_LAG + 1
 
 IDLE_VECTOR_COLS = 256
 BUSY_VECTOR_COLS = 64
@@ -43,18 +44,21 @@ def tile_attention_pa_kernel(tc, x, cos, sin, Wq, Wk, Wv, out_0, out_1, out_2):
         result_rows = result_4d.rearrange("b s h d -> (b s) (h d)")
         for col0 in range(0, weight.shape[1], GROUP_COLS):
             groups.append((weight, result_rows, col0, with_rope))
-    n_chunks = len(groups) * PASSES
     n_banks = len(groups) * TOKEN_TILES
+
+    chunks = [(group, c) for c in range(PASSES) for group in range(2)]
+    chunks += [(group, c) for group in range(2, len(groups)) for c in range(PASSES)]
+    n_chunks = len(chunks)
 
     with ExitStack() as ctx:
         ctx.enter_context(tc.manual_schedule())
         const = ctx.enter_context(tc.tile_pool(name="const", bufs=1))
         x_pool = ctx.enter_context(tc.tile_pool(name="x_rows", bufs=TOKEN_TILES))
-        raw_pool = ctx.enter_context(tc.tile_pool(name="raw", bufs=PREFETCH + 2))
+        raw_pool = ctx.enter_context(tc.tile_pool(name="raw", bufs=2 * PASSES))
         grouped_pool = ctx.enter_context(tc.tile_pool(name="grouped", bufs=4))
-        codes_pool = ctx.enter_context(tc.tile_pool(name="codes", bufs=6))
+        codes_pool = ctx.enter_context(tc.tile_pool(name="codes", bufs=8))
         rope_pool = ctx.enter_context(tc.tile_pool(name="rope", bufs=3))
-        result_pool = ctx.enter_context(tc.tile_pool(name="result", bufs=4))
+        result_pool = ctx.enter_context(tc.tile_pool(name="result", bufs=8))
         psum = ctx.enter_context(tc.psum_pool(name="psum", bufs=8))
 
         x_rows = x.rearrange("b s k -> (b s) k")
@@ -71,20 +75,20 @@ def tile_attention_pa_kernel(tc, x, cos, sin, Wq, Wk, Wv, out_0, out_1, out_2):
 
         raw_tiles = {}
 
-        def load(chunk):
-            weight, col0 = groups[chunk // PASSES][0], groups[chunk // PASSES][2]
-            k0 = (chunk % PASSES) * K_PASS
-            raw = raw_pool.tile([P, PACK, GROUP_COLS], BF16, name="raw")
+        def load(even_group, c):
+            weight, col0 = groups[even_group][0], groups[even_group][2]
+            raw = raw_pool.tile([P, PACK, PAIR_COLS], BF16, name="raw")
             nc.sync.dma_start(
                 out=raw[:],
-                in_=weight[k0 : k0 + K_PASS, col0 : col0 + GROUP_COLS].rearrange(
+                in_=weight[c * K_PASS : (c + 1) * K_PASS, col0 : col0 + PAIR_COLS].rearrange(
                     "(p j) w -> p j w", j=PACK
                 ),
             )
-            raw_tiles[chunk] = raw
+            raw_tiles[(even_group, c)] = raw[:, :, 0:GROUP_COLS]
+            raw_tiles[(even_group + 1, c)] = raw[:, :, GROUP_COLS:PAIR_COLS]
 
-        for chunk in range(PREFETCH):
-            load(chunk)
+        for c in range(PASSES):
+            load(0, c)
 
         identity = const.tile([P, P], F32, name="identity")
         make_identity(nc, identity[:])
@@ -151,7 +155,7 @@ def tile_attention_pa_kernel(tc, x, cos, sin, Wq, Wk, Wv, out_0, out_1, out_2):
             grouped_tiles[chunk] = grouped
 
         def quantise_and_multiply(chunk):
-            group, c = divmod(chunk, PASSES)
+            group, c = chunk
             grouped = grouped_tiles[chunk]
             w_codes = codes_pool.tile([P, GROUP_COLS], U32, name="w_codes", align_bytes=64)
             w_scales = codes_pool.tile([P, GROUP_COLS], U8, name="w_scales", align_bytes=64)
@@ -203,12 +207,12 @@ def tile_attention_pa_kernel(tc, x, cos, sin, Wq, Wk, Wv, out_0, out_1, out_2):
             nc.sync.dma_start(out=result_rows[t0 : t0 + P, col0 : col0 + GROUP_COLS], in_=result[:])
 
         for slot in range(n_banks + FINISH_LAG):
-            if slot + PREFETCH < n_chunks:
-                load(slot + PREFETCH)
+            if slot + PREFETCH < n_chunks and chunks[slot + PREFETCH][0] % 2 == 0:
+                load(chunks[slot + PREFETCH][0], chunks[slot + PREFETCH][1])
             if 0 <= slot - MULTIPLY_LAG < n_chunks:
-                quantise_and_multiply(slot - MULTIPLY_LAG)
+                quantise_and_multiply(chunks[slot - MULTIPLY_LAG])
             if slot < n_chunks:
-                regroup(slot, BUSY_VECTOR_COLS if has_rope(slot) else IDLE_VECTOR_COLS)
+                regroup(chunks[slot], BUSY_VECTOR_COLS if has_rope(slot) else IDLE_VECTOR_COLS)
 
             index = slot - FINISH_LAG
             if index >= 0:

@@ -23,14 +23,14 @@ HEAD = 128
 HALF = HEAD // 2
 GROUP_COLS = 512
 GROUP_HEADS = GROUP_COLS // HEAD
-PAIR_COLS = 2 * GROUP_COLS
 WORDS_PER_PASS = K_PASS // 2
 
 FLOPS = 2 * TOKENS * D_MODEL * (2048 + 1024 + 1024)
 
-PREFETCH = 2 * PASSES
+PREFETCH = 16
+RESULT_BUFS = 16
 MULTIPLY_LAG = 2
-FINISH_LAG = 2 * PASSES - 2 + MULTIPLY_LAG + 1
+FINISH_LAG = PASSES + MULTIPLY_LAG
 
 IDLE_VECTOR_COLS = 256
 BUSY_VECTOR_COLS = 64
@@ -44,21 +44,18 @@ def tile_attention_pa_kernel(tc, x, cos, sin, Wq, Wk, Wv, out_0, out_1, out_2):
         result_rows = result_4d.rearrange("b s h d -> (b s) (h d)")
         for col0 in range(0, weight.shape[1], GROUP_COLS):
             groups.append((weight, result_rows, col0, with_rope))
+    n_chunks = len(groups) * PASSES
     n_banks = len(groups) * TOKEN_TILES
-
-    chunks = [(group, c) for c in range(PASSES) for group in range(2)]
-    chunks += [(group, c) for group in range(2, len(groups)) for c in range(PASSES)]
-    n_chunks = len(chunks)
 
     with ExitStack() as ctx:
         ctx.enter_context(tc.manual_schedule())
         const = ctx.enter_context(tc.tile_pool(name="const", bufs=1))
         x_pool = ctx.enter_context(tc.tile_pool(name="x_rows", bufs=TOKEN_TILES))
-        raw_pool = ctx.enter_context(tc.tile_pool(name="raw", bufs=2 * PASSES))
+        raw_pool = ctx.enter_context(tc.tile_pool(name="raw", bufs=PREFETCH + 2))
         grouped_pool = ctx.enter_context(tc.tile_pool(name="grouped", bufs=4))
-        codes_pool = ctx.enter_context(tc.tile_pool(name="codes", bufs=8))
+        codes_pool = ctx.enter_context(tc.tile_pool(name="codes", bufs=6))
         rope_pool = ctx.enter_context(tc.tile_pool(name="rope", bufs=3))
-        result_pool = ctx.enter_context(tc.tile_pool(name="result", bufs=8))
+        result_pool = ctx.enter_context(tc.tile_pool(name="result", bufs=RESULT_BUFS))
         psum = ctx.enter_context(tc.psum_pool(name="psum", bufs=8))
 
         x_rows = x.rearrange("b s k -> (b s) k")
@@ -75,20 +72,20 @@ def tile_attention_pa_kernel(tc, x, cos, sin, Wq, Wk, Wv, out_0, out_1, out_2):
 
         raw_tiles = {}
 
-        def load(even_group, c):
-            weight, col0 = groups[even_group][0], groups[even_group][2]
-            raw = raw_pool.tile([P, PACK, PAIR_COLS], BF16, name="raw")
+        def load(chunk):
+            weight, col0 = groups[chunk // PASSES][0], groups[chunk // PASSES][2]
+            k0 = (chunk % PASSES) * K_PASS
+            raw = raw_pool.tile([P, PACK, GROUP_COLS], BF16, name="raw")
             nc.sync.dma_start(
                 out=raw[:],
-                in_=weight[c * K_PASS : (c + 1) * K_PASS, col0 : col0 + PAIR_COLS].rearrange(
+                in_=weight[k0 : k0 + K_PASS, col0 : col0 + GROUP_COLS].rearrange(
                     "(p j) w -> p j w", j=PACK
                 ),
             )
-            raw_tiles[(even_group, c)] = raw[:, :, 0:GROUP_COLS]
-            raw_tiles[(even_group + 1, c)] = raw[:, :, GROUP_COLS:PAIR_COLS]
+            raw_tiles[chunk] = raw
 
-        for c in range(PASSES):
-            load(0, c)
+        for chunk in range(PREFETCH):
+            load(chunk)
 
         identity = const.tile([P, P], F32, name="identity")
         make_identity(nc, identity[:])
@@ -155,7 +152,7 @@ def tile_attention_pa_kernel(tc, x, cos, sin, Wq, Wk, Wv, out_0, out_1, out_2):
             grouped_tiles[chunk] = grouped
 
         def quantise_and_multiply(chunk):
-            group, c = chunk
+            group, c = divmod(chunk, PASSES)
             grouped = grouped_tiles[chunk]
             w_codes = codes_pool.tile([P, GROUP_COLS], U32, name="w_codes", align_bytes=64)
             w_scales = codes_pool.tile([P, GROUP_COLS], U8, name="w_scales", align_bytes=64)
@@ -207,12 +204,12 @@ def tile_attention_pa_kernel(tc, x, cos, sin, Wq, Wk, Wv, out_0, out_1, out_2):
             nc.sync.dma_start(out=result_rows[t0 : t0 + P, col0 : col0 + GROUP_COLS], in_=result[:])
 
         for slot in range(n_banks + FINISH_LAG):
-            if slot + PREFETCH < n_chunks and chunks[slot + PREFETCH][0] % 2 == 0:
-                load(chunks[slot + PREFETCH][0], chunks[slot + PREFETCH][1])
+            if slot + PREFETCH < n_chunks:
+                load(slot + PREFETCH)
             if 0 <= slot - MULTIPLY_LAG < n_chunks:
-                quantise_and_multiply(chunks[slot - MULTIPLY_LAG])
+                quantise_and_multiply(slot - MULTIPLY_LAG)
             if slot < n_chunks:
-                regroup(chunks[slot], BUSY_VECTOR_COLS if has_rope(slot) else IDLE_VECTOR_COLS)
+                regroup(slot, BUSY_VECTOR_COLS if has_rope(slot) else IDLE_VECTOR_COLS)
 
             index = slot - FINISH_LAG
             if index >= 0:

@@ -90,13 +90,12 @@ def tile_attention_pa_kernel(tc, x, cos, sin, Wq, Wk, Wv, out_0, out_1, out_2):
         identity = const.tile([P, P], F32, name="identity")
         make_identity(nc, identity[:])
 
-        cos_f32 = const.tile([P, POSITION_TILES, HEAD], F32, name="cos_f32")
-        sin_signed = const.tile([P, POSITION_TILES, HEAD], F32, name="sin_signed")
-        nc.vector.tensor_copy(out=cos_f32[:], in_=cos_bf[:])
+        factors = const.tile([P, POSITION_TILES, 2, HEAD], F32, name="factors")
+        nc.vector.tensor_copy(out=factors[:, :, 0, :], in_=cos_bf[:])
+        nc.vector.tensor_copy(out=factors[:, :, 1, 0:HALF], in_=sin_bf[:, :, HALF:HEAD])
         nc.vector.tensor_scalar_mul(
-            out=sin_signed[:, :, 0:HALF], in0=sin_bf[:, :, 0:HALF], scalar1=-1.0
+            out=factors[:, :, 1, HALF:HEAD], in0=sin_bf[:, :, 0:HALF], scalar1=-1.0
         )
-        nc.vector.tensor_copy(out=sin_signed[:, :, HALF:HEAD], in_=sin_bf[:, :, HALF:HEAD])
 
         x_grouped = const.tile([P, TOKEN_TILES, PASSES, P, 2], F32, name="x_grouped", align_bytes=64)
         x_codes = const.tile([P, TOKEN_TILES, PASSES, P], U32, name="x_codes", align_bytes=64)
@@ -178,25 +177,17 @@ def tile_attention_pa_kernel(tc, x, cos, sin, Wq, Wk, Wv, out_0, out_1, out_2):
         def rope_products(index):
             bank = bank_tiles[index]
             pt = (index % TOKEN_TILES) % POSITION_TILES
-            direct = rope_pool.tile([P, GROUP_HEADS, HEAD], F32, name="direct")
-            crossed = rope_pool.tile([P, GROUP_HEADS, 2, HALF], F32, name="crossed")
+            products = rope_pool.tile([P, 2, GROUP_HEADS, HEAD], F32, name="products")
             nc.vector.tensor_tensor(
-                out=direct[:],
-                in0=bank[:].rearrange("p (h d) -> p h d", d=HEAD),
-                in1=cos_f32[:, pt, :].unsqueeze(1).to_broadcast([P, GROUP_HEADS, HEAD]),
+                out=products[:],
+                in0=bank[:]
+                .rearrange("p (h d) -> p h d", d=HEAD)
+                .unsqueeze(1)
+                .to_broadcast([P, 2, GROUP_HEADS, HEAD]),
+                in1=factors[:, pt].unsqueeze(2).to_broadcast([P, 2, GROUP_HEADS, HEAD]),
                 op=MULT,
             )
-            halves = bank[:].rearrange("p (h two d) -> p h two d", two=2, d=HALF)
-            for two in range(2):
-                nc.vector.tensor_tensor(
-                    out=crossed[:, :, two, :],
-                    in0=halves[:, :, 1 - two, :],
-                    in1=sin_signed[:, pt, two * HALF : (two + 1) * HALF]
-                    .unsqueeze(1)
-                    .to_broadcast([P, GROUP_HEADS, HALF]),
-                    op=MULT,
-                )
-            return direct, crossed
+            return products
 
         def store(index, result):
             result_rows, col0 = groups[index // TOKEN_TILES][1], groups[index // TOKEN_TILES][2]
@@ -215,11 +206,11 @@ def tile_attention_pa_kernel(tc, x, cos, sin, Wq, Wk, Wv, out_0, out_1, out_2):
             if index >= 0:
                 result = result_pool.tile([P, GROUP_COLS], F32, name="result")
                 if has_rope(slot):
-                    direct, crossed = rope_products(index)
+                    products = rope_products(index)
                     nc.gpsimd.tensor_tensor(
-                        out=result[:],
-                        in0=direct[:].rearrange("p h d -> p (h d)"),
-                        in1=crossed[:].rearrange("p h two d -> p (h two d)"),
+                        out=result[:].rearrange("p (h two d) -> p h two d", two=2, d=HALF),
+                        in0=products[:, 0].rearrange("p h (two d) -> p h two d", two=2),
+                        in1=products[:, 1].rearrange("p h (two d) -> p h two d", two=2)[:, :, ::-1, :],
                         op=ADD,
                     )
                 elif index % 2 == 0:

@@ -33,7 +33,7 @@ MULTIPLY_LAG = 2
 FINISH_LAG = PASSES + MULTIPLY_LAG
 
 IDLE_VECTOR_COLS = 256
-BUSY_VECTOR_COLS = 64
+BUSY_VECTOR_COLS = 96
 
 
 def tile_attention_pa_kernel(tc, x, cos, sin, Wq, Wk, Wv, out_0, out_1, out_2):

@@ -32,8 +32,11 @@ RESULT_BUFS = 16
 MULTIPLY_LAG = 2
 FINISH_LAG = PASSES + MULTIPLY_LAG
 
+THROUGH_FIRST = 6
+THROUGH_LAST = 24
+THROUGH_COLS = 128
 IDLE_VECTOR_COLS = 256
-BUSY_VECTOR_COLS = 96
+BUSY_VECTOR_COLS = 32
 
 
 def tile_attention_pa_kernel(tc, x, cos, sin, Wq, Wk, Wv, out_0, out_1, out_2):
@@ -53,7 +56,7 @@ def tile_attention_pa_kernel(tc, x, cos, sin, Wq, Wk, Wv, out_0, out_1, out_2):
         x_pool = ctx.enter_context(tc.tile_pool(name="x_rows", bufs=TOKEN_TILES))
         raw_pool = ctx.enter_context(tc.tile_pool(name="raw", bufs=PREFETCH + 2))
         grouped_pool = ctx.enter_context(tc.tile_pool(name="grouped", bufs=4))
-        codes_pool = ctx.enter_context(tc.tile_pool(name="codes", bufs=6))
+        codes_pool = ctx.enter_context(tc.tile_pool(name="codes", bufs=9))
         rope_pool = ctx.enter_context(tc.tile_pool(name="rope", bufs=3))
         result_pool = ctx.enter_context(tc.tile_pool(name="result", bufs=RESULT_BUFS))
         psum = ctx.enter_context(tc.psum_pool(name="psum", bufs=8))
@@ -89,6 +92,8 @@ def tile_attention_pa_kernel(tc, x, cos, sin, Wq, Wk, Wv, out_0, out_1, out_2):
 
         identity = const.tile([P, P], F32, name="identity")
         make_identity(nc, identity[:])
+        identity_bf = const.tile([P, P], BF16, name="identity_bf")
+        make_identity(nc, identity_bf[:])
 
         factors = const.tile([P, POSITION_TILES, 2, HEAD], F32, name="factors")
         nc.vector.tensor_copy(out=factors[:, :, 0, :], in_=cos_bf[:])
@@ -150,8 +155,40 @@ def tile_attention_pa_kernel(tc, x, cos, sin, Wq, Wk, Wv, out_0, out_1, out_2):
                     )
             grouped_tiles[chunk] = grouped
 
-        def quantise_and_multiply(chunk):
-            group, c = divmod(chunk, PASSES)
+        laid_tiles = {}
+        codes_tiles = {}
+
+        def goes_through(chunk):
+            return THROUGH_FIRST <= chunk <= THROUGH_LAST and chunk % 2 == 0
+
+        def lay_out(chunk):
+            raw = raw_tiles[chunk]
+            laid_tiles[chunk] = []
+            for half in range(2):
+                laid = psum.tile([P, 2, THROUGH_COLS, PACK], BF16, name="laid", tag="bank")
+                for part in range(2):
+                    w0 = (2 * half + part) * THROUGH_COLS
+                    nc.tensor.matmul(
+                        out=laid[:, part],
+                        lhsT=identity_bf[:],
+                        rhs=raw[:, :, w0 : w0 + THROUGH_COLS].rearrange("p j w -> p w j"),
+                        start=True,
+                        stop=True,
+                    )
+                laid_tiles[chunk].append(laid)
+
+        def collect(chunk):
+            grouped = grouped_pool.tile([P, GROUP_COLS, PACK], BF16, name="grouped", align_bytes=64)
+            for half in range(2):
+                nc.scalar.copy(
+                    out=grouped[:, half * 2 * THROUGH_COLS : (half + 1) * 2 * THROUGH_COLS, :].rearrange(
+                        "p w j -> p (w j)"
+                    ),
+                    in_=laid_tiles[chunk][half][:].rearrange("p a w j -> p (a w j)"),
+                )
+            grouped_tiles[chunk] = grouped
+
+        def quantise(chunk):
             grouped = grouped_tiles[chunk]
             w_codes = codes_pool.tile([P, GROUP_COLS], U32, name="w_codes", align_bytes=64)
             w_scales = codes_pool.tile([P, GROUP_COLS], U8, name="w_scales", align_bytes=64)
@@ -160,19 +197,23 @@ def tile_attention_pa_kernel(tc, x, cos, sin, Wq, Wk, Wv, out_0, out_1, out_2):
                 scales=w_scales[:],
                 in_=grouped[:].rearrange("p w j -> p (w j)"),
             )
-            for tt in range(TOKEN_TILES):
-                if c == 0:
-                    bank = psum.tile([P, GROUP_COLS], F32, name="bank", tag="bank")
-                    bank_tiles[group * TOKEN_TILES + tt] = bank
-                nc.tensor.matmul_mx(
-                    out=bank_tiles[group * TOKEN_TILES + tt][:],
-                    lhsT=x_codes[:, tt, c, :].bitcast(FP8X4),
-                    lhsT_scale=x_scales[:, tt, c, :],
-                    rhs=w_codes[:].bitcast(FP8X4),
-                    rhs_scale=w_scales[:],
-                    start=(c == 0),
-                    stop=(c == PASSES - 1),
-                )
+            codes_tiles[chunk] = (w_codes, w_scales)
+
+        def multiply(index, c):
+            group, tt = divmod(index, TOKEN_TILES)
+            w_codes, w_scales = codes_tiles[group * PASSES + c]
+            if c == 0:
+                bank = psum.tile([P, GROUP_COLS], F32, name="bank", tag="bank")
+                bank_tiles[index] = bank
+            nc.tensor.matmul_mx(
+                out=bank_tiles[index][:],
+                lhsT=x_codes[:, tt, c, :].bitcast(FP8X4),
+                lhsT_scale=x_scales[:, tt, c, :],
+                rhs=w_codes[:].bitcast(FP8X4),
+                rhs_scale=w_scales[:],
+                start=(c == 0),
+                stop=(c == PASSES - 1),
+            )
 
         def rope_products(index):
             bank = bank_tiles[index]
@@ -197,10 +238,23 @@ def tile_attention_pa_kernel(tc, x, cos, sin, Wq, Wk, Wv, out_0, out_1, out_2):
         for slot in range(n_banks + FINISH_LAG):
             if slot + PREFETCH < n_chunks:
                 load(slot + PREFETCH)
-            if 0 <= slot - MULTIPLY_LAG < n_chunks:
-                quantise_and_multiply(slot - MULTIPLY_LAG)
+            if goes_through(slot + 1):
+                lay_out(slot + 1)
+            ready = slot - MULTIPLY_LAG
+            if 0 <= ready < n_chunks:
+                quantise(ready)
+            coming = slot - FINISH_LAG + 1
+            if 0 <= coming < n_banks and groups[coming // TOKEN_TILES][3]:
+                for c in range(PASSES):
+                    multiply(coming, c)
+            if 0 <= ready < n_chunks and not groups[ready // PASSES][3]:
+                for tt in range(TOKEN_TILES):
+                    multiply((ready // PASSES) * TOKEN_TILES + tt, ready % PASSES)
             if slot < n_chunks:
-                regroup(slot, BUSY_VECTOR_COLS if has_rope(slot) else IDLE_VECTOR_COLS)
+                if goes_through(slot):
+                    collect(slot)
+                else:
+                    regroup(slot, BUSY_VECTOR_COLS if has_rope(slot) else IDLE_VECTOR_COLS)
 
             index = slot - FINISH_LAG
             if index >= 0:

@@ -32,11 +32,13 @@ RESULT_BUFS = 16
 MULTIPLY_LAG = 2
 FINISH_LAG = PASSES + MULTIPLY_LAG
 
-THROUGH_FIRST = 6
-THROUGH_LAST = 24
-THROUGH_COLS = 128
+THROUGH_GROUPS = (2, 3, 4, 5, 6)
+THROUGH_LEAD = 2
+THROUGH_COLS = 256
+THROUGH_WIDTH = 128
 IDLE_VECTOR_COLS = 256
-BUSY_VECTOR_COLS = 32
+BUSY_VECTOR_COLS = 64
+RELIEVED_VECTOR_COLS = 32
 
 
 def tile_attention_pa_kernel(tc, x, cos, sin, Wq, Wk, Wv, out_0, out_1, out_2):
@@ -55,7 +57,7 @@ def tile_attention_pa_kernel(tc, x, cos, sin, Wq, Wk, Wv, out_0, out_1, out_2):
         const = ctx.enter_context(tc.tile_pool(name="const", bufs=1))
         x_pool = ctx.enter_context(tc.tile_pool(name="x_rows", bufs=TOKEN_TILES))
         raw_pool = ctx.enter_context(tc.tile_pool(name="raw", bufs=PREFETCH + 2))
-        grouped_pool = ctx.enter_context(tc.tile_pool(name="grouped", bufs=4))
+        grouped_pool = ctx.enter_context(tc.tile_pool(name="grouped", bufs=5))
         codes_pool = ctx.enter_context(tc.tile_pool(name="codes", bufs=9))
         rope_pool = ctx.enter_context(tc.tile_pool(name="rope", bufs=3))
         result_pool = ctx.enter_context(tc.tile_pool(name="result", bufs=RESULT_BUFS))
@@ -159,19 +161,20 @@ def tile_attention_pa_kernel(tc, x, cos, sin, Wq, Wk, Wv, out_0, out_1, out_2):
         codes_tiles = {}
 
         def goes_through(chunk):
-            return THROUGH_FIRST <= chunk <= THROUGH_LAST and chunk % 2 == 0
+            return chunk % PASSES == 0 and chunk // PASSES in THROUGH_GROUPS
 
         def lay_out(chunk):
             raw = raw_tiles[chunk]
             laid_tiles[chunk] = []
-            for half in range(2):
-                laid = psum.tile([P, 2, THROUGH_COLS, PACK], BF16, name="laid", tag="bank")
-                for part in range(2):
-                    w0 = (2 * half + part) * THROUGH_COLS
+            for half in range(GROUP_COLS // THROUGH_COLS):
+                laid = psum.tile([P, THROUGH_COLS, PACK], BF16, name="laid", tag="bank")
+                for part in range(THROUGH_COLS // THROUGH_WIDTH):
+                    l0 = part * THROUGH_WIDTH
+                    w0 = half * THROUGH_COLS + l0
                     nc.tensor.matmul(
-                        out=laid[:, part],
+                        out=laid[:, l0 : l0 + THROUGH_WIDTH, :].rearrange("p (r i) j -> p r j i", i=4),
                         lhsT=identity_bf[:],
-                        rhs=raw[:, :, w0 : w0 + THROUGH_COLS].rearrange("p j w -> p w j"),
+                        rhs=raw[:, :, w0 : w0 + THROUGH_WIDTH].rearrange("p j (r i) -> p r j i", i=4),
                         start=True,
                         stop=True,
                     )
@@ -179,12 +182,12 @@ def tile_attention_pa_kernel(tc, x, cos, sin, Wq, Wk, Wv, out_0, out_1, out_2):
 
         def collect(chunk):
             grouped = grouped_pool.tile([P, GROUP_COLS, PACK], BF16, name="grouped", align_bytes=64)
-            for half in range(2):
+            for half in range(GROUP_COLS // THROUGH_COLS):
                 nc.scalar.copy(
-                    out=grouped[:, half * 2 * THROUGH_COLS : (half + 1) * 2 * THROUGH_COLS, :].rearrange(
+                    out=grouped[:, half * THROUGH_COLS : (half + 1) * THROUGH_COLS, :].rearrange(
                         "p w j -> p (w j)"
                     ),
-                    in_=laid_tiles[chunk][half][:].rearrange("p a w j -> p (a w j)"),
+                    in_=laid_tiles[chunk][half][:].rearrange("p w j -> p (w j)"),
                 )
             grouped_tiles[chunk] = grouped
 
@@ -238,8 +241,6 @@ def tile_attention_pa_kernel(tc, x, cos, sin, Wq, Wk, Wv, out_0, out_1, out_2):
         for slot in range(n_banks + FINISH_LAG):
             if slot + PREFETCH < n_chunks:
                 load(slot + PREFETCH)
-            if goes_through(slot + 1):
-                lay_out(slot + 1)
             ready = slot - MULTIPLY_LAG
             if 0 <= ready < n_chunks:
                 quantise(ready)
@@ -250,11 +251,17 @@ def tile_attention_pa_kernel(tc, x, cos, sin, Wq, Wk, Wv, out_0, out_1, out_2):
             if 0 <= ready < n_chunks and not groups[ready // PASSES][3]:
                 for tt in range(TOKEN_TILES):
                     multiply((ready // PASSES) * TOKEN_TILES + tt, ready % PASSES)
+            if goes_through(slot + THROUGH_LEAD):
+                lay_out(slot + THROUGH_LEAD)
             if slot < n_chunks:
                 if goes_through(slot):
                     collect(slot)
+                elif not has_rope(slot):
+                    regroup(slot, IDLE_VECTOR_COLS)
+                elif slot // PASSES in THROUGH_GROUPS:
+                    regroup(slot, RELIEVED_VECTOR_COLS)
                 else:
-                    regroup(slot, BUSY_VECTOR_COLS if has_rope(slot) else IDLE_VECTOR_COLS)
+                    regroup(slot, BUSY_VECTOR_COLS)
 
             index = slot - FINISH_LAG
             if index >= 0:

@@ -32,7 +32,7 @@ RESULT_BUFS = 16
 MULTIPLY_LAG = 2
 FINISH_LAG = PASSES + MULTIPLY_LAG
 
-THROUGH_GROUPS = (2, 3, 4, 5, 6)
+THROUGH_GROUPS = ()
 THROUGH_LEAD = 2
 THROUGH_COLS = 256
 THROUGH_WIDTH = 128
@@ -117,7 +117,7 @@ def tile_attention_pa_kernel(tc, x, cos, sin, Wq, Wk, Wv, out_0, out_1, out_2):
 
         for tt in range(TOKEN_TILES):
             x_words = x_tiles[tt][:].bitcast(F32)
-            for first_pass, copy_out in ((0, nc.scalar.copy), (2, nc.vector.tensor_copy)):
+            for first_pass, copy_out in ((0, nc.scalar.copy), (2, nc.scalar.copy)):
                 x_t = psum.tile([P, 2, 2, P], F32, name="x_t", tag="bank")
                 for c2 in range(2):
                     w0 = (first_pass + c2) * WORDS_PER_PASS

@@ -32,13 +32,10 @@ RESULT_BUFS = 16
 MULTIPLY_LAG = 2
 FINISH_LAG = PASSES + MULTIPLY_LAG
 
-THROUGH_GROUPS = ()
-THROUGH_LEAD = 2
-THROUGH_COLS = 256
-THROUGH_WIDTH = 128
 IDLE_VECTOR_COLS = 256
-BUSY_VECTOR_COLS = 64
-RELIEVED_VECTOR_COLS = 32
+BUSY_VECTOR_COLS = 0
+LAID_COLS = 128
+BANK_LAID_COLS = 256
 
 
 def tile_attention_pa_kernel(tc, x, cos, sin, Wq, Wk, Wv, out_0, out_1, out_2):
@@ -61,7 +58,8 @@ def tile_attention_pa_kernel(tc, x, cos, sin, Wq, Wk, Wv, out_0, out_1, out_2):
         codes_pool = ctx.enter_context(tc.tile_pool(name="codes", bufs=9))
         rope_pool = ctx.enter_context(tc.tile_pool(name="rope", bufs=3))
         result_pool = ctx.enter_context(tc.tile_pool(name="result", bufs=RESULT_BUFS))
-        psum = ctx.enter_context(tc.psum_pool(name="psum", bufs=8))
+        psum = ctx.enter_context(tc.psum_pool(name="psum", bufs=6))
+        laid_pool = ctx.enter_context(tc.psum_pool(name="laid_psum", bufs=2))
 
         x_rows = x.rearrange("b s k -> (b s) k")
         x_tiles = []
@@ -142,54 +140,41 @@ def tile_attention_pa_kernel(tc, x, cos, sin, Wq, Wk, Wv, out_0, out_1, out_2):
             bank = slot - FINISH_LAG
             return 0 <= bank < n_banks and groups[bank // TOKEN_TILES][3]
 
-        def regroup(chunk, vector_cols):
+        laid_tiles = {}
+
+        def lay_out(chunk):
+            laid = laid_pool.tile([P, BANK_LAID_COLS, PACK], BF16, name="laid")
+            nc.tensor.matmul(
+                out=laid[:, 0:LAID_COLS, :].rearrange("p w j -> p j w"),
+                lhsT=identity_bf[:],
+                rhs=raw_tiles[chunk][:, :, GROUP_COLS - LAID_COLS : GROUP_COLS],
+                start=True,
+                stop=True,
+            )
+            laid_tiles[chunk] = laid
+
+        def regroup(chunk, vector_cols, laid_cols):
             raw = raw_tiles[chunk]
             grouped = grouped_pool.tile([P, GROUP_COLS, PACK], BF16, name="grouped", align_bytes=64)
-            scalar_cols = GROUP_COLS - vector_cols
+            direct_cols = GROUP_COLS - laid_cols
+            scalar_cols = direct_cols - vector_cols
             for copy, w0, w1 in (
                 (nc.scalar.copy, 0, scalar_cols),
-                (nc.vector.tensor_copy, scalar_cols, GROUP_COLS),
+                (nc.vector.tensor_copy, scalar_cols, direct_cols),
             ):
                 if w1 > w0:
                     copy(
                         out=grouped[:, w0:w1, :].rearrange("p (r i) j -> p r j i", i=4),
                         in_=raw[:, :, w0:w1].rearrange("p j (r i) -> p r j i", i=4),
                     )
-            grouped_tiles[chunk] = grouped
-
-        laid_tiles = {}
-        codes_tiles = {}
-
-        def goes_through(chunk):
-            return chunk % PASSES == 0 and chunk // PASSES in THROUGH_GROUPS
-
-        def lay_out(chunk):
-            raw = raw_tiles[chunk]
-            laid_tiles[chunk] = []
-            for half in range(GROUP_COLS // THROUGH_COLS):
-                laid = psum.tile([P, THROUGH_COLS, PACK], BF16, name="laid", tag="bank")
-                for part in range(THROUGH_COLS // THROUGH_WIDTH):
-                    l0 = part * THROUGH_WIDTH
-                    w0 = half * THROUGH_COLS + l0
-                    nc.tensor.matmul(
-                        out=laid[:, l0 : l0 + THROUGH_WIDTH, :].rearrange("p (r i) j -> p r j i", i=4),
-                        lhsT=identity_bf[:],
-                        rhs=raw[:, :, w0 : w0 + THROUGH_WIDTH].rearrange("p j (r i) -> p r j i", i=4),
-                        start=True,
-                        stop=True,
-                    )
-                laid_tiles[chunk].append(laid)
-
-        def collect(chunk):
-            grouped = grouped_pool.tile([P, GROUP_COLS, PACK], BF16, name="grouped", align_bytes=64)
-            for half in range(GROUP_COLS // THROUGH_COLS):
+            if laid_cols > 0:
                 nc.scalar.copy(
-                    out=grouped[:, half * THROUGH_COLS : (half + 1) * THROUGH_COLS, :].rearrange(
-                        "p w j -> p (w j)"
-                    ),
-                    in_=laid_tiles[chunk][half][:].rearrange("p w j -> p (w j)"),
+                    out=grouped[:, direct_cols:GROUP_COLS, :].rearrange("p w j -> p (w j)"),
+                    in_=laid_tiles[chunk][:, 0:laid_cols, :].rearrange("p w j -> p (w j)"),
                 )
             grouped_tiles[chunk] = grouped
+
+        codes_tiles = {}
 
         def quantise(chunk):
             grouped = grouped_tiles[chunk]
@@ -245,23 +230,19 @@ def tile_attention_pa_kernel(tc, x, cos, sin, Wq, Wk, Wv, out_0, out_1, out_2):
             if 0 <= ready < n_chunks:
                 quantise(ready)
             coming = slot - FINISH_LAG + 1
-            if 0 <= coming < n_banks and groups[coming // TOKEN_TILES][3]:
+            if 0 <= coming < n_banks - TOKEN_TILES:
                 for c in range(PASSES):
                     multiply(coming, c)
-            if 0 <= ready < n_chunks and not groups[ready // PASSES][3]:
+            if n_chunks - PASSES <= ready < n_chunks:
                 for tt in range(TOKEN_TILES):
                     multiply((ready // PASSES) * TOKEN_TILES + tt, ready % PASSES)
-            if goes_through(slot + THROUGH_LEAD):
-                lay_out(slot + THROUGH_LEAD)
+            if slot + 1 < n_chunks and has_rope(slot + 1):
+                lay_out(slot + 1)
             if slot < n_chunks:
-                if goes_through(slot):
-                    collect(slot)
-                elif not has_rope(slot):
-                    regroup(slot, IDLE_VECTOR_COLS)
-                elif slot // PASSES in THROUGH_GROUPS:
-                    regroup(slot, RELIEVED_VECTOR_COLS)
+                if has_rope(slot):
+                    regroup(slot, BUSY_VECTOR_COLS, LAID_COLS)
                 else:
-                    regroup(slot, BUSY_VECTOR_COLS)
+                    regroup(slot, IDLE_VECTOR_COLS, 0)
 
             index = slot - FINISH_LAG
             if index >= 0:

@@ -35,6 +35,8 @@ FINISH_LAG = PASSES + MULTIPLY_LAG
 IDLE_VECTOR_COLS = 256
 BUSY_VECTOR_COLS = 0
 LAID_COLS = 128
+SCALAR_RUN = 8
+VECTOR_RUN = 4
 BANK_LAID_COLS = 256
 
 
@@ -158,14 +160,14 @@ def tile_attention_pa_kernel(tc, x, cos, sin, Wq, Wk, Wv, out_0, out_1, out_2):
             grouped = grouped_pool.tile([P, GROUP_COLS, PACK], BF16, name="grouped", align_bytes=64)
             direct_cols = GROUP_COLS - laid_cols
             scalar_cols = direct_cols - vector_cols
-            for copy, w0, w1 in (
-                (nc.scalar.copy, 0, scalar_cols),
-                (nc.vector.tensor_copy, scalar_cols, direct_cols),
+            for copy, run, w0, w1 in (
+                (nc.scalar.copy, SCALAR_RUN, 0, scalar_cols),
+                (nc.vector.tensor_copy, VECTOR_RUN, scalar_cols, direct_cols),
             ):
                 if w1 > w0:
                     copy(
-                        out=grouped[:, w0:w1, :].rearrange("p (r i) j -> p r j i", i=4),
-                        in_=raw[:, :, w0:w1].rearrange("p j (r i) -> p r j i", i=4),
+                        out=grouped[:, w0:w1, :].rearrange("p (r i) j -> p r j i", i=run),
+                        in_=raw[:, :, w0:w1].rearrange("p j (r i) -> p r j i", i=run),
                     )
             if laid_cols > 0:
                 nc.scalar.copy(

@@ -33,7 +33,7 @@ MULTIPLY_LAG = 2
 FINISH_LAG = PASSES + MULTIPLY_LAG
 
 IDLE_VECTOR_COLS = 256
-BUSY_VECTOR_COLS = 0
+BUSY_VECTOR_COLS = 24
 LAID_COLS = 128
 SCALAR_RUN = 8
 VECTOR_RUN = 4

@@ -33,7 +33,7 @@ MULTIPLY_LAG = 2
 FINISH_LAG = PASSES + MULTIPLY_LAG
 
 IDLE_VECTOR_COLS = 256
-BUSY_VECTOR_COLS = 24
+BUSY_VECTOR_COLS = (96, 0, 0, 0)
 LAID_COLS = 128
 SCALAR_RUN = 8
 VECTOR_RUN = 4
@@ -56,9 +56,9 @@ def tile_attention_pa_kernel(tc, x, cos, sin, Wq, Wk, Wv, out_0, out_1, out_2):
         const = ctx.enter_context(tc.tile_pool(name="const", bufs=1))
         x_pool = ctx.enter_context(tc.tile_pool(name="x_rows", bufs=TOKEN_TILES))
         raw_pool = ctx.enter_context(tc.tile_pool(name="raw", bufs=PREFETCH + 2))
-        grouped_pool = ctx.enter_context(tc.tile_pool(name="grouped", bufs=5))
+        grouped_pool = ctx.enter_context(tc.tile_pool(name="grouped", bufs=7))
         codes_pool = ctx.enter_context(tc.tile_pool(name="codes", bufs=9))
-        rope_pool = ctx.enter_context(tc.tile_pool(name="rope", bufs=3))
+        rope_pool = ctx.enter_context(tc.tile_pool(name="rope", bufs=2))
         result_pool = ctx.enter_context(tc.tile_pool(name="result", bufs=RESULT_BUFS))
         psum = ctx.enter_context(tc.psum_pool(name="psum", bufs=6))
         laid_pool = ctx.enter_context(tc.psum_pool(name="laid_psum", bufs=2))
@@ -177,6 +177,7 @@ def tile_attention_pa_kernel(tc, x, cos, sin, Wq, Wk, Wv, out_0, out_1, out_2):
             grouped_tiles[chunk] = grouped
 
         codes_tiles = {}
+        products_tiles = {}
 
         def quantise(chunk):
             grouped = grouped_tiles[chunk]
@@ -208,9 +209,12 @@ def tile_attention_pa_kernel(tc, x, cos, sin, Wq, Wk, Wv, out_0, out_1, out_2):
         def rope_products(index):
             bank = bank_tiles[index]
             pt = (index % TOKEN_TILES) % POSITION_TILES
-            products = rope_pool.tile([P, 2, GROUP_HEADS, HEAD], F32, name="products")
+            if index % TOKEN_TILES == 0:
+                products_of_group = rope_pool.tile([P, TOKEN_TILES, 2, GROUP_HEADS, HEAD], F32, name="products_of_group")
+                products_tiles[index // TOKEN_TILES] = products_of_group
+            products = products_tiles[index // TOKEN_TILES][:, index % TOKEN_TILES]
             nc.vector.tensor_tensor(
-                out=products[:],
+                out=products,
                 in0=bank[:]
                 .rearrange("p (h d) -> p h d", d=HEAD)
                 .unsqueeze(1)
@@ -242,7 +246,7 @@ def tile_attention_pa_kernel(tc, x, cos, sin, Wq, Wk, Wv, out_0, out_1, out_2):
                 lay_out(slot + 1)
             if slot < n_chunks:
                 if has_rope(slot):
-                    regroup(slot, BUSY_VECTOR_COLS, LAID_COLS)
+                    regroup(slot, BUSY_VECTOR_COLS[slot % PASSES], LAID_COLS)
                 else:
                     regroup(slot, IDLE_VECTOR_COLS, 0)
 

@@ -29,11 +29,11 @@ FLOPS = 2 * TOKENS * D_MODEL * (2048 + 1024 + 1024)
 
 PREFETCH = 16
 RESULT_BUFS = 16
-MULTIPLY_LAG = 2
-FINISH_LAG = PASSES + MULTIPLY_LAG
+FIRST_LAG = 1
+LAG = 2
 
-IDLE_VECTOR_COLS = 256
-BUSY_VECTOR_COLS = (96, 0, 0, 0)
+IDLE_VECTOR_COLS = 224
+BUSY_VECTOR_COLS = 96
 LAID_COLS = 128
 SCALAR_RUN = 8
 VECTOR_RUN = 4
@@ -50,6 +50,24 @@ def tile_attention_pa_kernel(tc, x, cos, sin, Wq, Wk, Wv, out_0, out_1, out_2):
             groups.append((weight, result_rows, col0, with_rope))
     n_chunks = len(groups) * PASSES
     n_banks = len(groups) * TOKEN_TILES
+    rope_banks = sum(group[3] for group in groups) * TOKEN_TILES
+    rope_chunks = rope_banks // TOKEN_TILES * PASSES
+
+    quantised_in = {}
+    for chunk in range(n_chunks):
+        slot = chunk + (FIRST_LAG if chunk < PASSES else LAG)
+        quantised_in.setdefault(slot, []).append(chunk)
+    finished_in = {}
+    for index in range(n_banks):
+        if index < TOKEN_TILES:
+            slot = index + PASSES + FIRST_LAG
+        elif rope_banks <= index < rope_banks + TOKEN_TILES:
+            slot = rope_banks + PASSES + LAG
+        else:
+            slot = index + PASSES + LAG
+        finished_in.setdefault(slot, []).append(index)
+    rope_slots = [slot for slot, indices in finished_in.items() if indices[0] < rope_banks]
+    n_slots = n_banks + PASSES + LAG
 
     with ExitStack() as ctx:
         ctx.enter_context(tc.manual_schedule())
@@ -72,8 +90,6 @@ def tile_attention_pa_kernel(tc, x, cos, sin, Wq, Wk, Wv, out_0, out_1, out_2):
 
         cos_bf = const.tile([P, POSITION_TILES, HEAD], BF16, name="cos_bf")
         sin_bf = const.tile([P, POSITION_TILES, HEAD], BF16, name="sin_bf")
-        nc.scalar.dma_start(out=cos_bf[:], in_=cos.rearrange("(h p) d -> p h d", p=P))
-        nc.scalar.dma_start(out=sin_bf[:], in_=sin.rearrange("(h p) d -> p h d", p=P))
 
         raw_tiles = {}
 
@@ -91,6 +107,9 @@ def tile_attention_pa_kernel(tc, x, cos, sin, Wq, Wk, Wv, out_0, out_1, out_2):
 
         for chunk in range(PREFETCH):
             load(chunk)
+            if chunk == PASSES:
+                nc.sync.dma_start(out=cos_bf[:], in_=cos.rearrange("(h p) d -> p h d", p=P))
+                nc.sync.dma_start(out=sin_bf[:], in_=sin.rearrange("(h p) d -> p h d", p=P))
 
         identity = const.tile([P, P], F32, name="identity")
         make_identity(nc, identity[:])
@@ -98,11 +117,13 @@ def tile_attention_pa_kernel(tc, x, cos, sin, Wq, Wk, Wv, out_0, out_1, out_2):
         make_identity(nc, identity_bf[:])
 
         factors = const.tile([P, POSITION_TILES, 2, HEAD], F32, name="factors")
-        nc.vector.tensor_copy(out=factors[:, :, 0, :], in_=cos_bf[:])
-        nc.vector.tensor_copy(out=factors[:, :, 1, 0:HALF], in_=sin_bf[:, :, HALF:HEAD])
-        nc.vector.tensor_scalar_mul(
-            out=factors[:, :, 1, HALF:HEAD], in0=sin_bf[:, :, 0:HALF], scalar1=-1.0
-        )
+
+        def make_factors():
+            nc.vector.tensor_copy(out=factors[:, :, 0, :], in_=cos_bf[:])
+            nc.vector.tensor_copy(out=factors[:, :, 1, 0:HALF], in_=sin_bf[:, :, HALF:HEAD])
+            nc.vector.tensor_scalar_mul(
+                out=factors[:, :, 1, HALF:HEAD], in0=sin_bf[:, :, 0:HALF], scalar1=-1.0
+            )
 
         x_grouped = const.tile([P, TOKEN_TILES, PASSES, P, 2], F32, name="x_grouped", align_bytes=64)
         x_codes = const.tile([P, TOKEN_TILES, PASSES, P], U32, name="x_codes", align_bytes=64)
@@ -117,7 +138,7 @@ def tile_attention_pa_kernel(tc, x, cos, sin, Wq, Wk, Wv, out_0, out_1, out_2):
 
         for tt in range(TOKEN_TILES):
             x_words = x_tiles[tt][:].bitcast(F32)
-            for first_pass, copy_out in ((0, nc.scalar.copy), (2, nc.scalar.copy)):
+            for first_pass, copy_out in ((0, nc.scalar.copy), (2, nc.vector.tensor_copy)):
                 x_t = psum.tile([P, 2, 2, P], F32, name="x_t", tag="bank")
                 for c2 in range(2):
                     w0 = (first_pass + c2) * WORDS_PER_PASS
@@ -137,10 +158,6 @@ def tile_attention_pa_kernel(tc, x, cos, sin, Wq, Wk, Wv, out_0, out_1, out_2):
 
         grouped_tiles = {}
         bank_tiles = {}
-
-        def has_rope(slot):
-            bank = slot - FINISH_LAG
-            return 0 <= bank < n_banks and groups[bank // TOKEN_TILES][3]
 
         laid_tiles = {}
 
@@ -229,31 +246,36 @@ def tile_attention_pa_kernel(tc, x, cos, sin, Wq, Wk, Wv, out_0, out_1, out_2):
             t0 = (index % TOKEN_TILES) * P
             nc.sync.dma_start(out=result_rows[t0 : t0 + P, col0 : col0 + GROUP_COLS], in_=result[:])
 
-        for slot in range(n_banks + FINISH_LAG):
-            if slot + PREFETCH < n_chunks:
-                load(slot + PREFETCH)
-            ready = slot - MULTIPLY_LAG
-            if 0 <= ready < n_chunks:
-                quantise(ready)
-            coming = slot - FINISH_LAG + 1
-            if 0 <= coming < n_banks - TOKEN_TILES:
-                for c in range(PASSES):
-                    multiply(coming, c)
-            if n_chunks - PASSES <= ready < n_chunks:
-                for tt in range(TOKEN_TILES):
-                    multiply((ready // PASSES) * TOKEN_TILES + tt, ready % PASSES)
-            if slot + 1 < n_chunks and has_rope(slot + 1):
-                lay_out(slot + 1)
-            if slot < n_chunks:
-                if has_rope(slot):
-                    regroup(slot, BUSY_VECTOR_COLS[slot % PASSES], LAID_COLS)
-                else:
-                    regroup(slot, IDLE_VECTOR_COLS, 0)
+        def lays_out(slot):
+            return slot in rope_slots and slot < rope_chunks + PASSES
 
-            index = slot - FINISH_LAG
-            if index >= 0:
+        def quantise_and_multiply(slot):
+            for chunk in quantised_in.get(slot, []):
+                quantise(chunk)
+            for index in finished_in.get(slot + 1, []):
+                if index < rope_banks:
+                    for c in range(PASSES):
+                        multiply(index, c)
+            for chunk in quantised_in.get(slot, []):
+                if chunk >= rope_chunks:
+                    for tt in range(TOKEN_TILES):
+                        multiply(chunk // PASSES * TOKEN_TILES + tt, chunk % PASSES)
+            if lays_out(slot + 1):
+                lay_out(slot + 1)
+
+        def regroup_in(slot):
+            if slot >= n_chunks:
+                return
+            laid_cols = LAID_COLS if lays_out(slot) else 0
+            if slot not in rope_slots:
+                regroup(slot, IDLE_VECTOR_COLS, laid_cols)
+            else:
+                regroup(slot, BUSY_VECTOR_COLS if slot % PASSES == 0 else 0, laid_cols)
+
+        def finish_in(slot):
+            for index in finished_in.get(slot, []):
                 result = result_pool.tile([P, GROUP_COLS], F32, name="result")
-                if has_rope(slot):
+                if index < rope_banks:
                     products = rope_products(index)
                     nc.gpsimd.tensor_tensor(
                         out=result[:].rearrange("p (h two d) -> p h two d", two=2, d=HALF),
@@ -266,3 +288,21 @@ def tile_attention_pa_kernel(tc, x, cos, sin, Wq, Wk, Wv, out_0, out_1, out_2):
                 else:
                     nc.vector.tensor_copy(out=result[:], in_=bank_tiles[index][:])
                 store(index, result)
+
+        first_rope_slot = min(rope_slots)
+        for slot in range(n_slots):
+            if slot + PREFETCH < n_chunks:
+                load(slot + PREFETCH)
+            if slot == first_rope_slot:
+                make_factors()
+            if slot < first_rope_slot:
+                regroup_in(slot)
+                quantise_and_multiply(slot)
+            elif slot <= max(rope_slots):
+                quantise_and_multiply(slot)
+                regroup_in(slot)
+                finish_in(slot)
+            else:
+                quantise_and_multiply(slot)
+                finish_in(slot)
+                regroup_in(slot)

@@ -28,12 +28,10 @@ WORDS_PER_PASS = K_PASS // 2
 FLOPS = 2 * TOKENS * D_MODEL * (2048 + 1024 + 1024)
 
 PREFETCH = 16
-RESULT_BUFS = 16
-FIRST_LAG = 1
-LAG = 2
-
-IDLE_VECTOR_COLS = 224
-BUSY_VECTOR_COLS = 96
+RESULT_BUFS = 8
+IDLE_VECTOR_COLS = 256
+TAIL_VECTOR_COLS = 320
+BUSY_VECTOR_COLS = 64
 LAID_COLS = 128
 SCALAR_RUN = 8
 VECTOR_RUN = 4
@@ -53,22 +51,6 @@ def tile_attention_pa_kernel(tc, x, cos, sin, Wq, Wk, Wv, out_0, out_1, out_2):
     rope_banks = sum(group[3] for group in groups) * TOKEN_TILES
     rope_chunks = rope_banks // TOKEN_TILES * PASSES
 
-    quantised_in = {}
-    for chunk in range(n_chunks):
-        slot = chunk + (FIRST_LAG if chunk < PASSES else LAG)
-        quantised_in.setdefault(slot, []).append(chunk)
-    finished_in = {}
-    for index in range(n_banks):
-        if index < TOKEN_TILES:
-            slot = index + PASSES + FIRST_LAG
-        elif rope_banks <= index < rope_banks + TOKEN_TILES:
-            slot = rope_banks + PASSES + LAG
-        else:
-            slot = index + PASSES + LAG
-        finished_in.setdefault(slot, []).append(index)
-    rope_slots = [slot for slot, indices in finished_in.items() if indices[0] < rope_banks]
-    n_slots = n_banks + PASSES + LAG
-
     with ExitStack() as ctx:
         ctx.enter_context(tc.manual_schedule())
         const = ctx.enter_context(tc.tile_pool(name="const", bufs=1))
@@ -76,7 +58,7 @@ def tile_attention_pa_kernel(tc, x, cos, sin, Wq, Wk, Wv, out_0, out_1, out_2):
         raw_pool = ctx.enter_context(tc.tile_pool(name="raw", bufs=PREFETCH + 2))
         grouped_pool = ctx.enter_context(tc.tile_pool(name="grouped", bufs=7))
         codes_pool = ctx.enter_context(tc.tile_pool(name="codes", bufs=9))
-        rope_pool = ctx.enter_context(tc.tile_pool(name="rope", bufs=2))
+        rope_pool = ctx.enter_context(tc.tile_pool(name="rope", bufs=4))
         result_pool = ctx.enter_context(tc.tile_pool(name="result", bufs=RESULT_BUFS))
         psum = ctx.enter_context(tc.psum_pool(name="psum", bufs=6))
         laid_pool = ctx.enter_context(tc.psum_pool(name="laid_psum", bufs=2))
@@ -194,7 +176,6 @@ def tile_attention_pa_kernel(tc, x, cos, sin, Wq, Wk, Wv, out_0, out_1, out_2):
             grouped_tiles[chunk] = grouped
 
         codes_tiles = {}
-        products_tiles = {}
 
         def quantise(chunk):
             grouped = grouped_tiles[chunk]
@@ -223,15 +204,11 @@ def tile_attention_pa_kernel(tc, x, cos, sin, Wq, Wk, Wv, out_0, out_1, out_2):
                 stop=(c == PASSES - 1),
             )
 
-        def rope_products(index):
+        def rope_products(products, index):
             bank = bank_tiles[index]
             pt = (index % TOKEN_TILES) % POSITION_TILES
-            if index % TOKEN_TILES == 0:
-                products_of_group = rope_pool.tile([P, TOKEN_TILES, 2, GROUP_HEADS, HEAD], F32, name="products_of_group")
-                products_tiles[index // TOKEN_TILES] = products_of_group
-            products = products_tiles[index // TOKEN_TILES][:, index % TOKEN_TILES]
             nc.vector.tensor_tensor(
-                out=products,
+                out=products[:, :, index % 2],
                 in0=bank[:]
                 .rearrange("p (h d) -> p h d", d=HEAD)
                 .unsqueeze(1)
@@ -239,70 +216,99 @@ def tile_attention_pa_kernel(tc, x, cos, sin, Wq, Wk, Wv, out_0, out_1, out_2):
                 in1=factors[:, pt].unsqueeze(2).to_broadcast([P, 2, GROUP_HEADS, HEAD]),
                 op=MULT,
             )
-            return products
 
-        def store(index, result):
-            result_rows, col0 = groups[index // TOKEN_TILES][1], groups[index // TOKEN_TILES][2]
-            t0 = (index % TOKEN_TILES) * P
-            nc.sync.dma_start(out=result_rows[t0 : t0 + P, col0 : col0 + GROUP_COLS], in_=result[:])
+        def store(first, result):
+            result_rows, col0 = groups[first // TOKEN_TILES][1], groups[first // TOKEN_TILES][2]
+            t0 = (first % TOKEN_TILES) * P
+            nc.sync.dma_start(
+                out=result_rows[t0 : t0 + result.shape[1] * P, col0 : col0 + GROUP_COLS].rearrange(
+                    "(i p) w -> p i w", p=P
+                ),
+                in_=result,
+            )
 
-        def lays_out(slot):
-            return slot in rope_slots and slot < rope_chunks + PASSES
+        def finish_ropes(first):
+            products = rope_pool.tile([P, 2, 2, GROUP_HEADS, HEAD], F32, name="products")
+            for index in (first, first + 1):
+                rope_products(products, index)
+            result = result_pool.tile([P, 2, GROUP_COLS], F32, name="result")
+            engine = nc.gpsimd if first < rope_banks - 2 else nc.vector
+            engine.tensor_tensor(
+                out=result[:].rearrange("p i (h two d) -> p (i h) two d", two=2, d=HALF),
+                in0=products[:, 0].rearrange("p i h (two d) -> p (i h) two d", two=2),
+                in1=products[:, 1].rearrange("p i h (two d) -> p (i h) two d", two=2)[:, :, ::-1, :],
+                op=ADD,
+            )
+            store(first, result[:])
 
-        def quantise_and_multiply(slot):
-            for chunk in quantised_in.get(slot, []):
+        def finish_values(first):
+            result = result_pool.tile([P, 2, GROUP_COLS], F32, name="result")
+            nc.scalar.copy(out=result[:, 0], in_=bank_tiles[first][:])
+            if first < n_banks - TOKEN_TILES:
+                nc.scalar.copy(out=result[:, 1], in_=bank_tiles[first + 1][:])
+                store(first, result[:])
+            else:
+                nc.vector.tensor_copy(out=result[:, 1], in_=bank_tiles[first + 1][:])
+                store(first, result[:, 0:1])
+                store(first + 1, result[:, 1:2])
+
+        n_steps = n_chunks // 2 + 2
+        finished_in = {}
+        for first in range(0, n_banks, 2):
+            if first < rope_banks:
+                step = first // 2 + 3
+            elif first < n_banks - TOKEN_TILES:
+                step = rope_banks // 2 + 3
+            else:
+                step = n_steps - 1
+            finished_in.setdefault(step, []).append(first)
+        rope_steps = [step for step, firsts in finished_in.items() if firsts[0] < rope_banks]
+
+        def lays_out(step):
+            return step in rope_steps and step <= rope_chunks // 2 + 1
+
+        def quantise_in(step):
+            if not 1 <= step <= n_chunks // 2:
+                return
+            for chunk in (2 * step - 2, 2 * step - 1):
                 quantise(chunk)
-            for index in finished_in.get(slot + 1, []):
-                if index < rope_banks:
-                    for c in range(PASSES):
-                        multiply(index, c)
-            for chunk in quantised_in.get(slot, []):
                 if chunk >= rope_chunks:
                     for tt in range(TOKEN_TILES):
                         multiply(chunk // PASSES * TOKEN_TILES + tt, chunk % PASSES)
-            if lays_out(slot + 1):
-                lay_out(slot + 1)
 
-        def regroup_in(slot):
-            if slot >= n_chunks:
+        def regroup_in(step):
+            if step >= n_chunks // 2:
                 return
-            laid_cols = LAID_COLS if lays_out(slot) else 0
-            if slot not in rope_slots:
-                regroup(slot, IDLE_VECTOR_COLS, laid_cols)
-            else:
-                regroup(slot, BUSY_VECTOR_COLS if slot % PASSES == 0 else 0, laid_cols)
-
-        def finish_in(slot):
-            for index in finished_in.get(slot, []):
-                result = result_pool.tile([P, GROUP_COLS], F32, name="result")
-                if index < rope_banks:
-                    products = rope_products(index)
-                    nc.gpsimd.tensor_tensor(
-                        out=result[:].rearrange("p (h two d) -> p h two d", two=2, d=HALF),
-                        in0=products[:, 0].rearrange("p h (two d) -> p h two d", two=2),
-                        in1=products[:, 1].rearrange("p h (two d) -> p h two d", two=2)[:, :, ::-1, :],
-                        op=ADD,
-                    )
-                elif index % 2 == 0:
-                    nc.scalar.copy(out=result[:], in_=bank_tiles[index][:])
+            for chunk in (2 * step, 2 * step + 1):
+                if step in rope_steps:
+                    vector_cols = BUSY_VECTOR_COLS if chunk % 2 == 0 else 0
                 else:
-                    nc.vector.tensor_copy(out=result[:], in_=bank_tiles[index][:])
-                store(index, result)
+                    vector_cols = IDLE_VECTOR_COLS if step < min(rope_steps) else TAIL_VECTOR_COLS
+                regroup(chunk, vector_cols, LAID_COLS if lays_out(step) else 0)
 
-        first_rope_slot = min(rope_slots)
-        for slot in range(n_slots):
-            if slot + PREFETCH < n_chunks:
-                load(slot + PREFETCH)
-            if slot == first_rope_slot:
+        for step in range(n_steps):
+            for chunk in (2 * step + PREFETCH, 2 * step + 1 + PREFETCH):
+                if chunk < n_chunks:
+                    load(chunk)
+            if step == min(rope_steps):
                 make_factors()
-            if slot < first_rope_slot:
-                regroup_in(slot)
-                quantise_and_multiply(slot)
-            elif slot <= max(rope_slots):
-                quantise_and_multiply(slot)
-                regroup_in(slot)
-                finish_in(slot)
-            else:
-                quantise_and_multiply(slot)
-                finish_in(slot)
-                regroup_in(slot)
+            if step < PASSES // 2:
+                regroup_in(step)
+            quantise_in(step)
+            for first in finished_in.get(step + 1, []):
+                if first < rope_banks:
+                    for index in (first, first + 1):
+                        for c in range(PASSES):
+                            multiply(index, c)
+            if lays_out(step + 1):
+                lay_out(2 * step + 2)
+                lay_out(2 * step + 3)
+            if PASSES // 2 <= step <= max(rope_steps):
+                regroup_in(step)
+            for first in finished_in.get(step, []):
+                if first < rope_banks:
+                    finish_ropes(first)
+                else:
+                    finish_values(first)
+            if step > max(rope_steps):
+                regroup_in(step)

from contextlib import ExitStack

import concourse.mybir as mybir
from concourse.masks import make_identity

F32 = mybir.dt.float32
BF16 = mybir.dt.bfloat16
U32 = mybir.dt.uint32
U8 = mybir.dt.uint8
FP8X4 = mybir.dt.float8_e4m3fn_x4
MULT = mybir.AluOpType.mult
ADD = mybir.AluOpType.add

P = 128
PACK = 4
K_PASS = P * PACK
TOKENS = 512
D_MODEL = 2048
PASSES = D_MODEL // K_PASS
TOKEN_TILES = TOKENS // P
POSITION_TILES = 256 // P
HEAD = 128
HALF = HEAD // 2
GROUP_COLS = 512
GROUP_HEADS = GROUP_COLS // HEAD
WORDS_PER_PASS = K_PASS // 2

FLOPS = 2 * TOKENS * D_MODEL * (2048 + 1024 + 1024)

PREFETCH = 16
RESULT_BUFS = 8
IDLE_VECTOR_COLS = 256
TAIL_VECTOR_COLS = 320
BUSY_VECTOR_COLS = 64
LAID_COLS = 128
SCALAR_RUN = 8
VECTOR_RUN = 4
BANK_LAID_COLS = 256


def tile_attention_pa_kernel(tc, x, cos, sin, Wq, Wk, Wv, out_0, out_1, out_2):
    nc = tc.nc

    groups = []
    for weight, result_4d, with_rope in ((Wq, out_0, True), (Wk, out_1, True), (Wv, out_2, False)):
        result_rows = result_4d.rearrange("b s h d -> (b s) (h d)")
        for col0 in range(0, weight.shape[1], GROUP_COLS):
            groups.append((weight, result_rows, col0, with_rope))
    n_chunks = len(groups) * PASSES
    n_banks = len(groups) * TOKEN_TILES
    rope_banks = sum(group[3] for group in groups) * TOKEN_TILES
    rope_chunks = rope_banks // TOKEN_TILES * PASSES

    with ExitStack() as ctx:
        ctx.enter_context(tc.manual_schedule())
        const = ctx.enter_context(tc.tile_pool(name="const", bufs=1))
        x_pool = ctx.enter_context(tc.tile_pool(name="x_rows", bufs=TOKEN_TILES))
        raw_pool = ctx.enter_context(tc.tile_pool(name="raw", bufs=PREFETCH + 2))
        grouped_pool = ctx.enter_context(tc.tile_pool(name="grouped", bufs=7))
        codes_pool = ctx.enter_context(tc.tile_pool(name="codes", bufs=9))
        rope_pool = ctx.enter_context(tc.tile_pool(name="rope", bufs=4))
        result_pool = ctx.enter_context(tc.tile_pool(name="result", bufs=RESULT_BUFS))
        psum = ctx.enter_context(tc.psum_pool(name="psum", bufs=6))
        laid_pool = ctx.enter_context(tc.psum_pool(name="laid_psum", bufs=2))

        x_rows = x.rearrange("b s k -> (b s) k")
        x_tiles = []
        for tt in range(TOKEN_TILES):
            x_sb = x_pool.tile([P, D_MODEL], BF16, name="x_sb")
            nc.sync.dma_start(out=x_sb[:], in_=x_rows[tt * P : (tt + 1) * P, :])
            x_tiles.append(x_sb)

        cos_bf = const.tile([P, POSITION_TILES, HEAD], BF16, name="cos_bf")
        sin_bf = const.tile([P, POSITION_TILES, HEAD], BF16, name="sin_bf")

        raw_tiles = {}

        def load(chunk):
            weight, col0 = groups[chunk // PASSES][0], groups[chunk // PASSES][2]
            k0 = (chunk % PASSES) * K_PASS
            raw = raw_pool.tile([P, PACK, GROUP_COLS], BF16, name="raw")
            nc.sync.dma_start(
                out=raw[:],
                in_=weight[k0 : k0 + K_PASS, col0 : col0 + GROUP_COLS].rearrange(
                    "(p j) w -> p j w", j=PACK
                ),
            )
            raw_tiles[chunk] = raw

        for chunk in range(PREFETCH):
            load(chunk)
            if chunk == PASSES:
                nc.sync.dma_start(out=cos_bf[:], in_=cos.rearrange("(h p) d -> p h d", p=P))
                nc.sync.dma_start(out=sin_bf[:], in_=sin.rearrange("(h p) d -> p h d", p=P))

        identity = const.tile([P, P], F32, name="identity")
        make_identity(nc, identity[:])
        identity_bf = const.tile([P, P], BF16, name="identity_bf")
        make_identity(nc, identity_bf[:])

        factors = const.tile([P, POSITION_TILES, 2, HEAD], F32, name="factors")

        def make_factors():
            nc.vector.tensor_copy(out=factors[:, :, 0, :], in_=cos_bf[:])
            nc.vector.tensor_copy(out=factors[:, :, 1, 0:HALF], in_=sin_bf[:, :, HALF:HEAD])
            nc.vector.tensor_scalar_mul(
                out=factors[:, :, 1, HALF:HEAD], in0=sin_bf[:, :, 0:HALF], scalar1=-1.0
            )

        x_grouped = const.tile([P, TOKEN_TILES, PASSES, P, 2], F32, name="x_grouped", align_bytes=64)
        x_codes = const.tile([P, TOKEN_TILES, PASSES, P], U32, name="x_codes", align_bytes=64)
        x_scales = const.tile([P, TOKEN_TILES, PASSES, P], U8, name="x_scales", align_bytes=64)

        def quantise_x(tt):
            nc.vector.quantize_mx(
                out=x_codes[:, tt].rearrange("p c t -> p (c t)").bitcast(FP8X4),
                scales=x_scales[:, tt].rearrange("p c t -> p (c t)"),
                in_=x_grouped[:, tt].rearrange("p c t u -> p (c t u)").bitcast(BF16),
            )

        for tt in range(TOKEN_TILES):
            x_words = x_tiles[tt][:].bitcast(F32)
            for first_pass, copy_out in ((0, nc.scalar.copy), (2, nc.vector.tensor_copy)):
                x_t = psum.tile([P, 2, 2, P], F32, name="x_t", tag="bank")
                for c2 in range(2):
                    w0 = (first_pass + c2) * WORDS_PER_PASS
                    for u in range(2):
                        nc.tensor.transpose(
                            out=x_t[:, c2, u, :],
                            in_=x_words[:, w0 + u : w0 + WORDS_PER_PASS : 2],
                            identity=identity[:],
                        )
                copy_out(
                    out=x_grouped[:, tt, first_pass : first_pass + 2],
                    in_=x_t[:].rearrange("p c u t -> p c t u"),
                )
            if tt > 0:
                quantise_x(tt - 1)
        quantise_x(TOKEN_TILES - 1)

        grouped_tiles = {}
        bank_tiles = {}

        laid_tiles = {}

        def lay_out(chunk):
            laid = laid_pool.tile([P, BANK_LAID_COLS, PACK], BF16, name="laid")
            nc.tensor.matmul(
                out=laid[:, 0:LAID_COLS, :].rearrange("p w j -> p j w"),
                lhsT=identity_bf[:],
                rhs=raw_tiles[chunk][:, :, GROUP_COLS - LAID_COLS : GROUP_COLS],
                start=True,
                stop=True,
            )
            laid_tiles[chunk] = laid

        def regroup(chunk, vector_cols, laid_cols):
            raw = raw_tiles[chunk]
            grouped = grouped_pool.tile([P, GROUP_COLS, PACK], BF16, name="grouped", align_bytes=64)
            direct_cols = GROUP_COLS - laid_cols
            scalar_cols = direct_cols - vector_cols
            for copy, run, w0, w1 in (
                (nc.scalar.copy, SCALAR_RUN, 0, scalar_cols),
                (nc.vector.tensor_copy, VECTOR_RUN, scalar_cols, direct_cols),
            ):
                if w1 > w0:
                    copy(
                        out=grouped[:, w0:w1, :].rearrange("p (r i) j -> p r j i", i=run),
                        in_=raw[:, :, w0:w1].rearrange("p j (r i) -> p r j i", i=run),
                    )
            if laid_cols > 0:
                nc.scalar.copy(
                    out=grouped[:, direct_cols:GROUP_COLS, :].rearrange("p w j -> p (w j)"),
                    in_=laid_tiles[chunk][:, 0:laid_cols, :].rearrange("p w j -> p (w j)"),
                )
            grouped_tiles[chunk] = grouped

        codes_tiles = {}

        def quantise(chunk):
            grouped = grouped_tiles[chunk]
            w_codes = codes_pool.tile([P, GROUP_COLS], U32, name="w_codes", align_bytes=64)
            w_scales = codes_pool.tile([P, GROUP_COLS], U8, name="w_scales", align_bytes=64)
            nc.vector.quantize_mx(
                out=w_codes[:].bitcast(FP8X4),
                scales=w_scales[:],
                in_=grouped[:].rearrange("p w j -> p (w j)"),
            )
            codes_tiles[chunk] = (w_codes, w_scales)

        def multiply(index, c):
            group, tt = divmod(index, TOKEN_TILES)
            w_codes, w_scales = codes_tiles[group * PASSES + c]
            if c == 0:
                bank = psum.tile([P, GROUP_COLS], F32, name="bank", tag="bank")
                bank_tiles[index] = bank
            nc.tensor.matmul_mx(
                out=bank_tiles[index][:],
                lhsT=x_codes[:, tt, c, :].bitcast(FP8X4),
                lhsT_scale=x_scales[:, tt, c, :],
                rhs=w_codes[:].bitcast(FP8X4),
                rhs_scale=w_scales[:],
                start=(c == 0),
                stop=(c == PASSES - 1),
            )

        def rope_products(products, index):
            bank = bank_tiles[index]
            pt = (index % TOKEN_TILES) % POSITION_TILES
            nc.vector.tensor_tensor(
                out=products[:, :, index % 2],
                in0=bank[:]
                .rearrange("p (h d) -> p h d", d=HEAD)
                .unsqueeze(1)
                .to_broadcast([P, 2, GROUP_HEADS, HEAD]),
                in1=factors[:, pt].unsqueeze(2).to_broadcast([P, 2, GROUP_HEADS, HEAD]),
                op=MULT,
            )

        def store(first, result):
            result_rows, col0 = groups[first // TOKEN_TILES][1], groups[first // TOKEN_TILES][2]
            t0 = (first % TOKEN_TILES) * P
            nc.sync.dma_start(
                out=result_rows[t0 : t0 + result.shape[1] * P, col0 : col0 + GROUP_COLS].rearrange(
                    "(i p) w -> p i w", p=P
                ),
                in_=result,
            )

        def finish_ropes(first):
            products = rope_pool.tile([P, 2, 2, GROUP_HEADS, HEAD], F32, name="products")
            for index in (first, first + 1):
                rope_products(products, index)
            result = result_pool.tile([P, 2, GROUP_COLS], F32, name="result")
            engine = nc.gpsimd if first < rope_banks - 2 else nc.vector
            engine.tensor_tensor(
                out=result[:].rearrange("p i (h two d) -> p (i h) two d", two=2, d=HALF),
                in0=products[:, 0].rearrange("p i h (two d) -> p (i h) two d", two=2),
                in1=products[:, 1].rearrange("p i h (two d) -> p (i h) two d", two=2)[:, :, ::-1, :],
                op=ADD,
            )
            store(first, result[:])

        def finish_values(first):
            result = result_pool.tile([P, 2, GROUP_COLS], F32, name="result")
            nc.scalar.copy(out=result[:, 0], in_=bank_tiles[first][:])
            if first < n_banks - TOKEN_TILES:
                nc.scalar.copy(out=result[:, 1], in_=bank_tiles[first + 1][:])
                store(first, result[:])
            else:
                nc.vector.tensor_copy(out=result[:, 1], in_=bank_tiles[first + 1][:])
                store(first, result[:, 0:1])
                store(first + 1, result[:, 1:2])

        n_steps = n_chunks // 2 + 2
        finished_in = {}
        for first in range(0, n_banks, 2):
            if first < rope_banks:
                step = first // 2 + 3
            elif first < n_banks - TOKEN_TILES:
                step = rope_banks // 2 + 3
            else:
                step = n_steps - 1
            finished_in.setdefault(step, []).append(first)
        rope_steps = [step for step, firsts in finished_in.items() if firsts[0] < rope_banks]

        def lays_out(step):
            return step in rope_steps and step <= rope_chunks // 2 + 1

        def quantise_in(step):
            if not 1 <= step <= n_chunks // 2:
                return
            for chunk in (2 * step - 2, 2 * step - 1):
                quantise(chunk)
                if chunk >= rope_chunks:
                    for tt in range(TOKEN_TILES):
                        multiply(chunk // PASSES * TOKEN_TILES + tt, chunk % PASSES)

        def regroup_in(step):
            if step >= n_chunks // 2:
                return
            for chunk in (2 * step, 2 * step + 1):
                if step in rope_steps:
                    vector_cols = BUSY_VECTOR_COLS if chunk % 2 == 0 else 0
                else:
                    vector_cols = IDLE_VECTOR_COLS if step < min(rope_steps) else TAIL_VECTOR_COLS
                regroup(chunk, vector_cols, LAID_COLS if lays_out(step) else 0)

        for step in range(n_steps):
            for chunk in (2 * step + PREFETCH, 2 * step + 1 + PREFETCH):
                if chunk < n_chunks:
                    load(chunk)
            if step == min(rope_steps):
                make_factors()
            if step < PASSES // 2:
                regroup_in(step)
            quantise_in(step)
            for first in finished_in.get(step + 1, []):
                if first < rope_banks:
                    for index in (first, first + 1):
                        for c in range(PASSES):
                            multiply(index, c)
            if lays_out(step + 1):
                lay_out(2 * step + 2)
                lay_out(2 * step + 3)
            if PASSES // 2 <= step <= max(rope_steps):
                regroup_in(step)
            for first in finished_in.get(step, []):
                if first < rope_banks:
                    finish_ropes(first)
                else:
                    finish_values(first)
            if step > max(rope_steps):
                regroup_in(step)
